import numpy as np
import ml_dtypes


BF16 = ml_dtypes.bfloat16


def bf(x):
    return np.asarray(x, np.float32).astype(BF16)


def f64(x):
    return np.asarray(x).astype(np.float64)


E2M1 = np.array([0.0, 0.5, 1.0, 1.5, 2.0, 3.0, 4.0, 6.0, -0.0, -0.5, -1.0, -1.5, -2.0, -3.0, -4.0, -6.0])


def pack_weight(w, fmt):
    k, n = w.shape
    w = f64(bf(w)).reshape(k // 32, 32, n)
    amax = np.abs(w).max(1)
    if fmt == "e4m3":
        byte = np.frexp(amax)[1] - 1 + 127 - 7
    else:
        mant, ex = np.frexp(amax / 6.0)
        byte = np.where(mant > 0.5, ex, ex - 1) + 127
    byte = np.clip(np.where(amax > 0, byte, 1), 1, 254)
    scaled = (w * np.exp2(127.0 - byte)[:, None, :]).reshape(k, n).astype(np.float32)
    by_word = np.ascontiguousarray(scaled.reshape(k // 512, 128, 4, n).transpose(0, 1, 3, 2))
    if fmt == "e4m3":
        words = by_word.astype(ml_dtypes.float8_e4m3fn).view(np.uint8)
    else:
        c = by_word.astype(ml_dtypes.float4_e2m1fn).view(np.uint8) & 0xF
        words = c[..., 0::2] | (c[..., 1::2] << 4)
    return np.ascontiguousarray(words), np.ascontiguousarray(byte.astype(np.uint8).reshape(k // 512, 16, n))


def unpack_weight(words, scales, fmt):
    g, p, n, _ = words.shape
    if fmt == "e4m3":
        vals = np.ascontiguousarray(words).view(ml_dtypes.float8_e4m3fn).astype(np.float64)
    else:
        nib = np.empty((g, p, n, 4), np.uint8)
        nib[..., 0::2] = words & 0xF
        nib[..., 1::2] = words >> 4
        vals = E2M1[nib]
    vals = vals * np.repeat(np.exp2(scales.astype(np.float64) - 127.0), 8, axis=1)[..., None]
    return vals.transpose(0, 1, 3, 2).reshape(g * 512, n)

def pack4(w):
    words, scales = pack_weight(w, "e2m1")
    return words.reshape(words.shape[0], 128, -1), scales


def unpack4(words, scales):
    return unpack_weight(words.reshape(words.shape[0], 128, -1, 2), scales, "e2m1")


def kspread(k):
    return np.exp2(np.repeat(np.random.randint(-6, 7, k // 32), 32).astype(np.float64))


B, S, H, N_HEADS, N_KV, D, QB, ORIG_MAX_POS = 1, 2048, 4096, 16, 4, 128, 512, 8192
ROPE_BASE = 5.0e5
ROPE_FACTOR = 8.0
LOW_FREQ, HIGH_FREQ = 1.0, 4.0


def llama3_cos_sin():
    inv_freq = 1.0 / (ROPE_BASE ** (np.arange(0, D, 2) / D))
    wavelen = 2.0 * np.pi / inv_freq
    smooth = np.clip((ORIG_MAX_POS / wavelen - LOW_FREQ) / (HIGH_FREQ - LOW_FREQ), 0.0, 1.0)
    new_inv_freq = (1.0 - smooth) * (inv_freq / ROPE_FACTOR) + smooth * inv_freq
    freqs = np.arange(S)[:, None] * new_inv_freq[None, :]
    emb = np.concatenate([freqs, freqs], axis=-1)
    return np.cos(emb), np.sin(emb)


def rotate_half(x):
    x1, x2 = x[..., : D // 2], x[..., D // 2:]
    return np.concatenate([-x2, x1], axis=-1)


def apply_rope(x, cos, sin):
    return x * cos[None, None, :, :] + rotate_half(x) * sin[None, None, :, :]


def setup_inputs():
    s = kspread(H)
    hidden_states = np.random.standard_normal((B, S, H)) * s
    wq = np.random.standard_normal((N_HEADS * D, H)) / np.sqrt(H) / s[None, :]
    wk = np.random.standard_normal((N_KV * D, H)) / np.sqrt(H) / s[None, :]
    hidden_states_words, hidden_states_scales = pack4(np.ascontiguousarray(hidden_states.reshape(B * S, H).T))
    wq_words, wq_scales = pack4(np.ascontiguousarray(wq.T))
    wk_words, wk_scales = pack4(np.ascontiguousarray(wk.T))
    return {"hidden_states_words": hidden_states_words, "hidden_states_scales": hidden_states_scales,
            "wq_words": wq_words, "wq_scales": wq_scales,
            "wk_words": wk_words, "wk_scales": wk_scales}


def reference(hidden_states_words, hidden_states_scales, wq_words, wq_scales, wk_words, wk_scales):
    xq = unpack4(hidden_states_words, hidden_states_scales).T.reshape(B, S, H)
    q = (xq @ unpack4(wq_words, wq_scales)).reshape(B, S, N_HEADS, D).transpose(0, 2, 1, 3)
    k = (xq @ unpack4(wk_words, wk_scales)).reshape(B, S, N_KV, D).transpose(0, 2, 1, 3)
    cos, sin = llama3_cos_sin()
    return apply_rope(q, cos, sin), apply_rope(k, cos, sin)

@@ -1,0 +1,264 @@
+from contextlib import ExitStack
+
+import concourse.mybir as mybir
+
+F32 = mybir.dt.float32
+BF16 = mybir.dt.bfloat16
+I32 = mybir.dt.int32
+U8 = mybir.dt.uint8
+FP4X4 = mybir.dt.float4_e2m1fn_x4
+ALU = mybir.AluOpType
+ACT = mybir.ActivationFunctionType
+
+P = 128
+TOKENS = 2048
+HIDDEN = 4096
+PASSES = HIDDEN // 512
+HEAD = 128
+HALF_D = HEAD // 2
+N_BLOCK = 512
+Q_BLOCKS = 4
+BLOCKS = 5
+TILES = TOKENS // P
+HALF_TILES = 8
+HALF_TOK = HALF_TILES * P
+
+PI = 3.141592653589793
+ROPE_BASE = 5.0e5
+
+FLOPS = 2 * TOKENS * (BLOCKS * N_BLOCK) * HIDDEN
+
+N_WARM = 6
+FIRST_RUNS = ((0, 2), (2, 5), (5, 8))
+TAIL_PIECES = ((0, 256), (256, 128), (384, 128))
+
+
+def tile_stickyllamaattention_pa_kernel(
+    tc,
+    hidden_states_words,
+    hidden_states_scales,
+    wq_words,
+    wq_scales,
+    wk_words,
+    wk_scales,
+    out_0,
+    out_1,
+):
+    nc = tc.nc
+
+    with ExitStack() as ctx:
+        keep = ctx.enter_context(tc.tile_pool(name="keep", bufs=1))
+        work = ctx.enter_context(tc.tile_pool(name="work", bufs=4))
+        psum = ctx.enter_context(tc.psum_pool(name="psum", bufs=8))
+        ctx.enter_context(tc.manual_schedule())
+
+        codes = {}
+        planes = {}
+
+        def source(kind, chunk):
+            if kind == "h":
+                return hidden_states_words, hidden_states_scales, chunk * HALF_TOK, HALF_TOK
+            if chunk < Q_BLOCKS:
+                return wq_words, wq_scales, chunk * N_BLOCK, N_BLOCK
+            return wk_words, wk_scales, 0, N_BLOCK
+
+        def make_plane(kind, chunk, g0, g1):
+            cols = source(kind, chunk)[3]
+            plane = keep.tile([P, g1 - g0, cols], U8, name="pl_%s%d_%d" % (kind, chunk, g0), align_bytes=64)
+            nc.vector.memset(plane[:].rearrange("p g c -> p (g c)").bitcast(I32), 0)
+            for g in range(g0, g1):
+                planes[(kind, chunk, g)] = plane[:, g - g0, :]
+            return plane
+
+        def load_scale_rows(plane, kind, chunk, g0, g1, quad):
+            scales, c0, cols = source(kind, chunk)[1:]
+            nc.sync.dma_start(
+                out=plane[32 * quad : 32 * quad + 4, :, :].bitcast(I32),
+                in_=scales[g0:g1, 4 * quad : 4 * quad + 4, c0 : c0 + cols].rearrange("g r n -> r g n").bitcast(I32),
+            )
+
+        def load_codes(kind, chunk, g0, g1):
+            words, unused, c0, cols = source(kind, chunk)
+            tile = keep.tile([P, g1 - g0, 2 * cols], U8, name="cd_%s%d_%d" % (kind, chunk, g0), align_bytes=64)
+            nc.sync.dma_start(
+                out=tile[:].bitcast(I32),
+                in_=words[g0:g1, :, 2 * c0 : 2 * (c0 + cols)].rearrange("g p c -> p g c").bitcast(I32),
+            )
+            for g in range(g0, g1):
+                codes[(kind, chunk, g)] = tile[:, g - g0, :]
+
+        zeros = keep.tile([P, N_BLOCK], BF16, name="zeros")
+        nc.vector.memset(zeros[:].bitcast(I32), 0)
+
+        g0, g1 = FIRST_RUNS[0]
+        w_plane = make_plane("w", 0, g0, g1)
+        h_plane = make_plane("h", 0, g0, g1)
+        load_scale_rows(w_plane, "w", 0, g0, g1, 0)
+        load_scale_rows(w_plane, "w", 0, g0, g1, 1)
+        load_codes("w", 0, 0, 1)
+        load_codes("h", 0, 0, 1)
+        load_scale_rows(w_plane, "w", 0, g0, g1, 2)
+        load_scale_rows(w_plane, "w", 0, g0, g1, 3)
+        for quad in range(4):
+            load_scale_rows(h_plane, "h", 0, g0, g1, quad)
+        for g in range(1, g1):
+            load_codes("w", 0, g, g + 1)
+            load_codes("h", 0, g, g + 1)
+        for g0, g1 in FIRST_RUNS[1:]:
+            w_plane = make_plane("w", 0, g0, g1)
+            h_plane = make_plane("h", 0, g0, g1)
+            for quad in range(4):
+                load_scale_rows(w_plane, "w", 0, g0, g1, quad)
+            for quad in range(4):
+                load_scale_rows(h_plane, "h", 0, g0, g1, quad)
+            for g in range(g0, g1):
+                load_codes("w", 0, g, g + 1)
+                load_codes("h", 0, g, g + 1)
+
+        warm = psum.tile([P, N_BLOCK], F32, name="warm", tag="acc")
+        for i in range(N_WARM):
+            nc.tensor.matmul(out=warm[:], lhsT=zeros[:, 0:P], rhs=zeros[:], start=True, stop=True)
+
+        pos_i = keep.tile([P, TILES], I32, name="pos_i")
+        nc.gpsimd.iota(pos_i[:], pattern=[[P, TILES]], base=0, channel_multiplier=1)
+        inv = keep.tile([P, HALF_D], F32, name="inv")
+        nc.vector.memset(inv[:, 0:1], 1.0)
+        scratch = keep.tile([P, 1], F32, name="scratch")
+        nc.scalar.activation(out=scratch[:], in_=inv[:, 0:1], func=ACT.Sin)
+        pos_f = keep.tile([P, TILES], F32, name="pos_f")
+
+        later = [("w", 1), ("w", 2), ("w", 3), ("w", 4), ("h", 1)]
+
+        def load_later(kind, chunk):
+            plane = make_plane(kind, chunk, 0, PASSES)
+            for quad in range(4):
+                load_scale_rows(plane, kind, chunk, 0, PASSES, quad)
+            for g in range(0, PASSES, 4):
+                load_codes(kind, chunk, g, g + 4)
+
+        m = 1
+        while m < HALF_D:
+            nc.vector.tensor_scalar(
+                out=inv[:, m : 2 * m], in0=inv[:, 0:m], scalar1=ROPE_BASE ** (-m / 64.0), scalar2=None, op0=ALU.mult
+            )
+            if later:
+                kind, chunk = later[0]
+                later.remove(later[0])
+                load_later(kind, chunk)
+            m *= 2
+        nc.vector.tensor_copy(out=pos_f[:], in_=pos_i[:])
+        smooth_raw = keep.tile([P, HALF_D], F32, name="smooth_raw")
+        nc.vector.tensor_scalar(
+            out=smooth_raw[:], in0=inv[:], scalar1=8192.0 / (6.0 * PI), scalar2=-1.0 / 3.0, op0=ALU.mult, op1=ALU.add
+        )
+        smooth = keep.tile([P, HALF_D], F32, name="smooth")
+        nc.vector.tensor_scalar(out=smooth[:], in0=smooth_raw[:], scalar1=0.0, scalar2=1.0, op0=ALU.max, op1=ALU.min)
+        gain = keep.tile([P, HALF_D], F32, name="gain")
+        nc.vector.tensor_scalar(
+            out=gain[:], in0=smooth[:], scalar1=7.0 / (16.0 * PI), scalar2=1.0 / (16.0 * PI), op0=ALU.mult, op1=ALU.add
+        )
+        turns_per_pos = keep.tile([P, HALF_D], F32, name="turns_per_pos")
+        nc.vector.tensor_tensor(out=turns_per_pos[:], in0=inv[:], in1=gain[:], op=ALU.mult)
+
+        table_shape = [P, TILES, HALF_D]
+        turns = keep.tile(table_shape, F32, name="turns")
+        nc.vector.tensor_tensor(
+            out=turns[:],
+            in0=pos_f[:].unsqueeze(2).to_broadcast(table_shape),
+            in1=turns_per_pos[:].unsqueeze(1).to_broadcast(table_shape),
+            op=ALU.mult,
+        )
+        flat = "p i j -> p (i j)"
+        whole_s = keep.tile(table_shape, I32, name="whole_s")
+        nc.vector.tensor_copy(out=whole_s[:], in_=turns[:])
+        frac_s = keep.tile(table_shape, F32, name="frac_s")
+        nc.vector.tensor_tensor(out=frac_s[:], in0=turns[:], in1=whole_s[:], op=ALU.subtract)
+        sin_t = keep.tile(table_shape, F32, name="sin_t")
+        nc.scalar.activation(out=sin_t[:], in_=frac_s[:], func=ACT.Sin, scale=2.0 * PI)
+        nsin_t = keep.tile(table_shape, F32, name="nsin_t")
+        nc.scalar.activation(out=nsin_t[:], in_=frac_s[:], func=ACT.Sin, scale=-2.0 * PI)
+        whole_c = keep.tile(table_shape, I32, name="whole_c")
+        nc.vector.tensor_scalar(out=whole_c[:], in0=turns[:], scalar1=0.25, scalar2=None, op0=ALU.add)
+        frac_c = keep.tile(table_shape, F32, name="frac_c")
+        nc.vector.scalar_tensor_tensor(
+            out=frac_c[:].rearrange(flat),
+            in0=turns[:].rearrange(flat),
+            scalar=0.25,
+            in1=whole_c[:].rearrange(flat),
+            op0=ALU.add,
+            op1=ALU.subtract,
+        )
+        cos_t = keep.tile(table_shape, F32, name="cos_t")
+        nc.scalar.activation(out=cos_t[:], in_=frac_c[:], func=ACT.Sin, scale=2.0 * PI)
+
+        def one_pass(acc, tok_tile, block, c0, width, g):
+            half, m_in = divmod(tok_tile, HALF_TILES)
+            nc.tensor.matmul_mx(
+                out=acc[:],
+                lhsT=codes[("h", half, g)][:, 2 * P * m_in : 2 * P * (m_in + 1)].bitcast(FP4X4),
+                lhsT_scale=planes[("h", half, g)][:, P * m_in : P * (m_in + 1)],
+                rhs=codes[("w", block, g)][:, 2 * c0 : 2 * (c0 + width)].bitcast(FP4X4),
+                rhs_scale=planes[("w", block, g)][:, c0 : c0 + width],
+                start=(g == 0),
+                stop=(g == PASSES - 1),
+            )
+
+        def epilogue(acc, tok_tile, block, c0, width, add_engine):
+            heads = width // HEAD
+            x_halves = acc[:].rearrange("p (a d) -> p a d", d=HALF_D)
+            x_heads = acc[:].rearrange("p (h u d) -> p h u d", u=2, d=HALF_D)
+            direct = work.tile([P, width], F32, name="direct", tag="direct")
+            nc.vector.tensor_tensor(
+                out=direct[:].rearrange("p (a d) -> p a d", d=HALF_D),
+                in0=x_halves,
+                in1=cos_t[:, tok_tile, :].unsqueeze(1).to_broadcast([P, 2 * heads, HALF_D]),
+                op=ALU.mult,
+            )
+            crossed = work.tile([P, width], F32, name="crossed", tag="crossed")
+            c_heads = crossed[:].rearrange("p (h u d) -> p h u d", u=2, d=HALF_D)
+            nc.vector.tensor_tensor(
+                out=c_heads[:, :, 0, :],
+                in0=x_heads[:, :, 1, :],
+                in1=nsin_t[:, tok_tile, :].unsqueeze(1).to_broadcast([P, heads, HALF_D]),
+                op=ALU.mult,
+            )
+            nc.vector.tensor_tensor(
+                out=c_heads[:, :, 1, :],
+                in0=x_heads[:, :, 0, :],
+                in1=sin_t[:, tok_tile, :].unsqueeze(1).to_broadcast([P, heads, HALF_D]),
+                op=ALU.mult,
+            )
+            result = work.tile([P, width], F32, name="result", tag="result", bufs=6)
+            add_engine.tensor_tensor(out=result[:], in0=direct[:], in1=crossed[:], op=ALU.add)
+            if block < Q_BLOCKS:
+                dest, h0 = out_0, (block * N_BLOCK + c0) // HEAD
+            else:
+                dest, h0 = out_1, c0 // HEAD
+            nc.scalar.dma_start(
+                out=dest[0, h0 : h0 + heads, tok_tile * P : (tok_tile + 1) * P, :].rearrange("h t d -> t h d"),
+                in_=result[:].rearrange("p (h d) -> p h d", d=HEAD),
+            )
+
+        first = []
+        for tok_tile in range(HALF_TILES):
+            acc = psum.tile([P, N_BLOCK], F32, name="acc%d" % tok_tile, tag="acc")
+            first.append(acc)
+        for g in range(PASSES):
+            for tok_tile in range(HALF_TILES):
+                one_pass(first[tok_tile], tok_tile, 0, 0, N_BLOCK, g)
+        for tok_tile in range(HALF_TILES):
+            epilogue(first[tok_tile], tok_tile, 0, 0, N_BLOCK, nc.gpsimd)
+
+        for half in range(2):
+            for block in range(BLOCKS):
+                if half == 0 and block == 0:
+                    continue
+                for m_in in range(HALF_TILES):
+                    tok_tile = half * HALF_TILES + m_in
+                    last = half == 1 and block == BLOCKS - 1 and m_in == HALF_TILES - 1
+                    pieces = TAIL_PIECES if last else ((0, N_BLOCK),)
+                    for c0, width in pieces:
+                        acc = psum.tile([P, width], F32, name="acc", tag="acc")
+                        for g in range(PASSES):
+                            one_pass(acc, tok_tile, block, c0, width, g)
+                        epilogue(acc, tok_tile, block, c0, width, nc.vector if last else nc.gpsimd)

@@ -28,7 +28,7 @@ ROPE_BASE = 5.0e5
 
 FLOPS = 2 * TOKENS * (BLOCKS * N_BLOCK) * HIDDEN
 
-N_WARM = 6
+N_WARM = 8
 FIRST_RUNS = ((0, 2), (2, 5), (5, 8))
 TAIL_PIECES = ((0, 256), (256, 128), (384, 128))
 
@@ -88,7 +88,7 @@ def tile_stickyllamaattention_pa_kernel(
                 codes[(kind, chunk, g)] = tile[:, g - g0, :]
 
         zeros = keep.tile([P, N_BLOCK], BF16, name="zeros")
-        nc.vector.memset(zeros[:].bitcast(I32), 0)
+        nc.gpsimd.memset(zeros[:], 0.0)
 
         g0, g1 = FIRST_RUNS[0]
         w_plane = make_plane("w", 0, g0, g1)
@@ -257,8 +257,11 @@ def tile_stickyllamaattention_pa_kernel(
                     tok_tile = half * HALF_TILES + m_in
                     last = half == 1 and block == BLOCKS - 1 and m_in == HALF_TILES - 1
                     pieces = TAIL_PIECES if last else ((0, N_BLOCK),)
+                    if half == 1 and block == BLOCKS - 1 and m_in == HALF_TILES - 2:
+                        pieces = ((0, 256), (256, 256))
                     for c0, width in pieces:
                         acc = psum.tile([P, width], F32, name="acc", tag="acc")
                         for g in range(PASSES):
                             one_pass(acc, tok_tile, block, c0, width, g)
-                        epilogue(acc, tok_tile, block, c0, width, nc.vector if last else nc.gpsimd)
+                        final = last and c0 + width == N_BLOCK
+                        epilogue(acc, tok_tile, block, c0, width, nc.vector if final else nc.gpsimd)

@@ -48,6 +48,7 @@ def tile_stickyllamaattention_pa_kernel(
 
     with ExitStack() as ctx:
         keep = ctx.enter_context(tc.tile_pool(name="keep", bufs=1))
+        small = ctx.enter_context(tc.tile_pool(name="small", bufs=1))
         work = ctx.enter_context(tc.tile_pool(name="work", bufs=4))
         psum = ctx.enter_context(tc.psum_pool(name="psum", bufs=8))
         ctx.enter_context(tc.manual_schedule())
@@ -64,7 +65,7 @@ def tile_stickyllamaattention_pa_kernel(
 
         def make_plane(kind, chunk, g0, g1):
             cols = source(kind, chunk)[3]
-            plane = keep.tile([P, g1 - g0, cols], U8, name="pl_%s%d_%d" % (kind, chunk, g0), align_bytes=64)
+            plane = keep.tile([P, g1 - g0, cols], U8, name="pl_%s%d_%d" % (kind, chunk, g0), align_bytes=256)
             nc.vector.memset(plane[:].rearrange("p g c -> p (g c)").bitcast(I32), 0)
             for g in range(g0, g1):
                 planes[(kind, chunk, g)] = plane[:, g - g0, :]
@@ -79,7 +80,7 @@ def tile_stickyllamaattention_pa_kernel(
 
         def load_codes(kind, chunk, g0, g1):
             words, unused, c0, cols = source(kind, chunk)
-            tile = keep.tile([P, g1 - g0, 2 * cols], U8, name="cd_%s%d_%d" % (kind, chunk, g0), align_bytes=64)
+            tile = keep.tile([P, g1 - g0, 2 * cols], U8, name="cd_%s%d_%d" % (kind, chunk, g0), align_bytes=256)
             nc.sync.dma_start(
                 out=tile[:].bitcast(I32),
                 in_=words[g0:g1, :, 2 * c0 : 2 * (c0 + cols)].rearrange("g p c -> p g c").bitcast(I32),
@@ -87,7 +88,7 @@ def tile_stickyllamaattention_pa_kernel(
             for g in range(g0, g1):
                 codes[(kind, chunk, g)] = tile[:, g - g0, :]
 
-        zeros = keep.tile([P, N_BLOCK], BF16, name="zeros")
+        zeros = small.tile([P, N_BLOCK], BF16, name="zeros")
         nc.gpsimd.memset(zeros[:], 0.0)
 
         g0, g1 = FIRST_RUNS[0]
@@ -119,13 +120,13 @@ def tile_stickyllamaattention_pa_kernel(
         for i in range(N_WARM):
             nc.tensor.matmul(out=warm[:], lhsT=zeros[:, 0:P], rhs=zeros[:], start=True, stop=True)
 
-        pos_i = keep.tile([P, TILES], I32, name="pos_i")
+        pos_i = small.tile([P, TILES], I32, name="pos_i")
         nc.gpsimd.iota(pos_i[:], pattern=[[P, TILES]], base=0, channel_multiplier=1)
-        inv = keep.tile([P, HALF_D], F32, name="inv")
+        inv = small.tile([P, HALF_D], F32, name="inv")
         nc.vector.memset(inv[:, 0:1], 1.0)
-        scratch = keep.tile([P, 1], F32, name="scratch")
+        scratch = small.tile([P, 1], F32, name="scratch")
         nc.scalar.activation(out=scratch[:], in_=inv[:, 0:1], func=ACT.Sin)
-        pos_f = keep.tile([P, TILES], F32, name="pos_f")
+        pos_f = small.tile([P, TILES], F32, name="pos_f")
 
         later = [("w", 1), ("w", 2), ("w", 3), ("w", 4), ("h", 1)]
 
@@ -147,21 +148,21 @@ def tile_stickyllamaattention_pa_kernel(
                 load_later(kind, chunk)
             m *= 2
         nc.vector.tensor_copy(out=pos_f[:], in_=pos_i[:])
-        smooth_raw = keep.tile([P, HALF_D], F32, name="smooth_raw")
+        smooth_raw = small.tile([P, HALF_D], F32, name="smooth_raw")
         nc.vector.tensor_scalar(
             out=smooth_raw[:], in0=inv[:], scalar1=8192.0 / (6.0 * PI), scalar2=-1.0 / 3.0, op0=ALU.mult, op1=ALU.add
         )
-        smooth = keep.tile([P, HALF_D], F32, name="smooth")
+        smooth = small.tile([P, HALF_D], F32, name="smooth")
         nc.vector.tensor_scalar(out=smooth[:], in0=smooth_raw[:], scalar1=0.0, scalar2=1.0, op0=ALU.max, op1=ALU.min)
-        gain = keep.tile([P, HALF_D], F32, name="gain")
+        gain = small.tile([P, HALF_D], F32, name="gain")
         nc.vector.tensor_scalar(
             out=gain[:], in0=smooth[:], scalar1=7.0 / (16.0 * PI), scalar2=1.0 / (16.0 * PI), op0=ALU.mult, op1=ALU.add
         )
-        turns_per_pos = keep.tile([P, HALF_D], F32, name="turns_per_pos")
+        turns_per_pos = small.tile([P, HALF_D], F32, name="turns_per_pos")
         nc.vector.tensor_tensor(out=turns_per_pos[:], in0=inv[:], in1=gain[:], op=ALU.mult)
 
         table_shape = [P, TILES, HALF_D]
-        turns = keep.tile(table_shape, F32, name="turns")
+        turns = small.tile(table_shape, F32, name="turns")
         nc.vector.tensor_tensor(
             out=turns[:],
             in0=pos_f[:].unsqueeze(2).to_broadcast(table_shape),
@@ -169,17 +170,17 @@ def tile_stickyllamaattention_pa_kernel(
             op=ALU.mult,
         )
         flat = "p i j -> p (i j)"
-        whole_s = keep.tile(table_shape, I32, name="whole_s")
+        whole_s = small.tile(table_shape, I32, name="whole_s")
         nc.vector.tensor_copy(out=whole_s[:], in_=turns[:])
-        frac_s = keep.tile(table_shape, F32, name="frac_s")
+        frac_s = small.tile(table_shape, F32, name="frac_s")
         nc.vector.tensor_tensor(out=frac_s[:], in0=turns[:], in1=whole_s[:], op=ALU.subtract)
-        sin_t = keep.tile(table_shape, F32, name="sin_t")
+        sin_t = small.tile(table_shape, F32, name="sin_t")
         nc.scalar.activation(out=sin_t[:], in_=frac_s[:], func=ACT.Sin, scale=2.0 * PI)
-        nsin_t = keep.tile(table_shape, F32, name="nsin_t")
+        nsin_t = small.tile(table_shape, F32, name="nsin_t")
         nc.scalar.activation(out=nsin_t[:], in_=frac_s[:], func=ACT.Sin, scale=-2.0 * PI)
-        whole_c = keep.tile(table_shape, I32, name="whole_c")
+        whole_c = small.tile(table_shape, I32, name="whole_c")
         nc.vector.tensor_scalar(out=whole_c[:], in0=turns[:], scalar1=0.25, scalar2=None, op0=ALU.add)
-        frac_c = keep.tile(table_shape, F32, name="frac_c")
+        frac_c = small.tile(table_shape, F32, name="frac_c")
         nc.vector.scalar_tensor_tensor(
             out=frac_c[:].rearrange(flat),
             in0=turns[:].rearrange(flat),
@@ -188,7 +189,7 @@ def tile_stickyllamaattention_pa_kernel(
             op0=ALU.add,
             op1=ALU.subtract,
         )
-        cos_t = keep.tile(table_shape, F32, name="cos_t")
+        cos_t = small.tile(table_shape, F32, name="cos_t")
         nc.scalar.activation(out=cos_t[:], in_=frac_c[:], func=ACT.Sin, scale=2.0 * PI)
 
         def one_pass(acc, tok_tile, block, c0, width, g):

@@ -28,7 +28,7 @@ ROPE_BASE = 5.0e5
 
 FLOPS = 2 * TOKENS * (BLOCKS * N_BLOCK) * HIDDEN
 
-N_WARM = 8
+N_WARM = 0
 FIRST_RUNS = ((0, 2), (2, 5), (5, 8))
 TAIL_PIECES = ((0, 256), (256, 128), (384, 128))
 

@@ -28,7 +28,7 @@ ROPE_BASE = 5.0e5
 
 FLOPS = 2 * TOKENS * (BLOCKS * N_BLOCK) * HIDDEN
 
-N_WARM = 0
+N_WARM = 8
 FIRST_RUNS = ((0, 2), (2, 5), (5, 8))
 TAIL_PIECES = ((0, 256), (256, 128), (384, 128))
 
@@ -78,30 +78,36 @@ def tile_stickyllamaattention_pa_kernel(
                 in_=scales[g0:g1, 4 * quad : 4 * quad + 4, c0 : c0 + cols].rearrange("g r n -> r g n").bitcast(I32),
             )
 
-        def load_codes(kind, chunk, g0, g1):
+        def load_codes(kind, chunk, g0, g1, first_col=0, n_cols=None):
             words, unused, c0, cols = source(kind, chunk)
-            tile = keep.tile([P, g1 - g0, 2 * cols], U8, name="cd_%s%d_%d" % (kind, chunk, g0), align_bytes=256)
+            c0 += first_col
+            if n_cols is not None:
+                cols = n_cols
+            tile = keep.tile([P, g1 - g0, 2 * cols], U8, name="cd_%s%d_%d_%d" % (kind, chunk, g0, first_col), align_bytes=256)
             nc.sync.dma_start(
                 out=tile[:].bitcast(I32),
                 in_=words[g0:g1, :, 2 * c0 : 2 * (c0 + cols)].rearrange("g p c -> p g c").bitcast(I32),
             )
             for g in range(g0, g1):
-                codes[(kind, chunk, g)] = tile[:, g - g0, :]
+                if kind == "w":
+                    codes[("w", chunk, g)] = tile[:, g - g0, :]
+                else:
+                    for i in range(cols // P):
+                        codes[("h", c0 // P + i, g)] = tile[:, g - g0, 2 * P * i : 2 * P * (i + 1)]
 
         zeros = small.tile([P, N_BLOCK], BF16, name="zeros")
         nc.gpsimd.memset(zeros[:], 0.0)
 
+        load_codes("w", 0, 0, 1)
+        load_codes("h", 0, 0, 1, 0, HALF_TOK // 2)
         g0, g1 = FIRST_RUNS[0]
         w_plane = make_plane("w", 0, g0, g1)
         h_plane = make_plane("h", 0, g0, g1)
-        load_scale_rows(w_plane, "w", 0, g0, g1, 0)
-        load_scale_rows(w_plane, "w", 0, g0, g1, 1)
-        load_codes("w", 0, 0, 1)
-        load_codes("h", 0, 0, 1)
-        load_scale_rows(w_plane, "w", 0, g0, g1, 2)
-        load_scale_rows(w_plane, "w", 0, g0, g1, 3)
+        for quad in range(4):
+            load_scale_rows(w_plane, "w", 0, g0, g1, quad)
         for quad in range(4):
             load_scale_rows(h_plane, "h", 0, g0, g1, quad)
+        load_codes("h", 0, 0, 1, HALF_TOK // 2, HALF_TOK // 2)
         for g in range(1, g1):
             load_codes("w", 0, g, g + 1)
             load_codes("h", 0, g, g + 1)
@@ -196,7 +202,7 @@ def tile_stickyllamaattention_pa_kernel(
             half, m_in = divmod(tok_tile, HALF_TILES)
             nc.tensor.matmul_mx(
                 out=acc[:],
-                lhsT=codes[("h", half, g)][:, 2 * P * m_in : 2 * P * (m_in + 1)].bitcast(FP4X4),
+                lhsT=codes[("h", tok_tile, g)].bitcast(FP4X4),
                 lhsT_scale=planes[("h", half, g)][:, P * m_in : P * (m_in + 1)],
                 rhs=codes[("w", block, g)][:, 2 * c0 : 2 * (c0 + width)].bitcast(FP4X4),
                 rhs_scale=planes[("w", block, g)][:, c0 : c0 + width],

@@ -180,10 +180,9 @@ def tile_stickyllamaattention_pa_kernel(
         nc.vector.tensor_copy(out=whole_s[:], in_=turns[:])
         frac_s = small.tile(table_shape, F32, name="frac_s")
         nc.vector.tensor_tensor(out=frac_s[:], in0=turns[:], in1=whole_s[:], op=ALU.subtract)
-        sin_t = small.tile(table_shape, F32, name="sin_t")
-        nc.scalar.activation(out=sin_t[:], in_=frac_s[:], func=ACT.Sin, scale=2.0 * PI)
-        nsin_t = small.tile(table_shape, F32, name="nsin_t")
-        nc.scalar.activation(out=nsin_t[:], in_=frac_s[:], func=ACT.Sin, scale=-2.0 * PI)
+        signed_sin = small.tile([P, TILES, 2, HALF_D], F32, name="signed_sin")
+        nc.scalar.activation(out=signed_sin[:, :, 1, :], in_=frac_s[:], func=ACT.Sin, scale=2.0 * PI)
+        nc.scalar.activation(out=signed_sin[:, :, 0, :], in_=frac_s[:], func=ACT.Sin, scale=-2.0 * PI)
         whole_c = small.tile(table_shape, I32, name="whole_c")
         nc.vector.tensor_scalar(out=whole_c[:], in0=turns[:], scalar1=0.25, scalar2=None, op0=ALU.add)
         frac_c = small.tile(table_shape, F32, name="frac_c")
@@ -222,17 +221,10 @@ def tile_stickyllamaattention_pa_kernel(
                 op=ALU.mult,
             )
             crossed = work.tile([P, width], F32, name="crossed", tag="crossed")
-            c_heads = crossed[:].rearrange("p (h u d) -> p h u d", u=2, d=HALF_D)
             nc.vector.tensor_tensor(
-                out=c_heads[:, :, 0, :],
-                in0=x_heads[:, :, 1, :],
-                in1=nsin_t[:, tok_tile, :].unsqueeze(1).to_broadcast([P, heads, HALF_D]),
-                op=ALU.mult,
-            )
-            nc.vector.tensor_tensor(
-                out=c_heads[:, :, 1, :],
-                in0=x_heads[:, :, 0, :],
-                in1=sin_t[:, tok_tile, :].unsqueeze(1).to_broadcast([P, heads, HALF_D]),
+                out=crossed[:].rearrange("p (h u d) -> p h u d", u=2, d=HALF_D),
+                in0=x_heads[:, :, ::-1, :],
+                in1=signed_sin[:, tok_tile, :, :].unsqueeze(1).to_broadcast([P, heads, 2, HALF_D]),
                 op=ALU.mult,
             )
             result = work.tile([P, width], F32, name="result", tag="result", bufs=6)

@@ -99,7 +99,7 @@ def tile_stickyllamaattention_pa_kernel(
         nc.gpsimd.memset(zeros[:], 0.0)
 
         load_codes("w", 0, 0, 1)
-        load_codes("h", 0, 0, 1, 0, HALF_TOK // 2)
+        load_codes("h", 0, 0, 1, 0, HALF_TOK // 4)
         g0, g1 = FIRST_RUNS[0]
         w_plane = make_plane("w", 0, g0, g1)
         h_plane = make_plane("h", 0, g0, g1)
@@ -107,6 +107,7 @@ def tile_stickyllamaattention_pa_kernel(
             load_scale_rows(w_plane, "w", 0, g0, g1, quad)
         for quad in range(4):
             load_scale_rows(h_plane, "h", 0, g0, g1, quad)
+        load_codes("h", 0, 0, 1, HALF_TOK // 4, HALF_TOK // 4)
         load_codes("h", 0, 0, 1, HALF_TOK // 2, HALF_TOK // 2)
         for g in range(1, g1):
             load_codes("w", 0, g, g + 1)
@@ -233,7 +234,8 @@ def tile_stickyllamaattention_pa_kernel(
                 dest, h0 = out_0, (block * N_BLOCK + c0) // HEAD
             else:
                 dest, h0 = out_1, c0 // HEAD
-            nc.scalar.dma_start(
+            store_queue = nc.sync if add_engine is nc.vector else nc.scalar
+            store_queue.dma_start(
                 out=dest[0, h0 : h0 + heads, tok_tile * P : (tok_tile + 1) * P, :].rearrange("h t d -> t h d"),
                 in_=result[:].rearrange("p (h d) -> p h d", d=HEAD),
             )

@@ -210,7 +210,7 @@ def tile_stickyllamaattention_pa_kernel(
                 stop=(g == PASSES - 1),
             )
 
-        def epilogue(acc, tok_tile, block, c0, width, add_engine):
+        def products(acc, tok_tile, width):
             heads = width // HEAD
             x_halves = acc[:].rearrange("p (a d) -> p a d", d=HALF_D)
             x_heads = acc[:].rearrange("p (h u d) -> p h u d", u=2, d=HALF_D)
@@ -228,13 +228,17 @@ def tile_stickyllamaattention_pa_kernel(
                 in1=signed_sin[:, tok_tile, :, :].unsqueeze(1).to_broadcast([P, heads, 2, HALF_D]),
                 op=ALU.mult,
             )
+            return direct, crossed
+
+        def finish(pair, tok_tile, block, c0, width, add_engine, store_queue):
+            heads = width // HEAD
+            direct, crossed = pair
             result = work.tile([P, width], F32, name="result", tag="result", bufs=6)
             add_engine.tensor_tensor(out=result[:], in0=direct[:], in1=crossed[:], op=ALU.add)
             if block < Q_BLOCKS:
                 dest, h0 = out_0, (block * N_BLOCK + c0) // HEAD
             else:
                 dest, h0 = out_1, c0 // HEAD
-            store_queue = nc.sync if add_engine is nc.vector else nc.scalar
             store_queue.dma_start(
                 out=dest[0, h0 : h0 + heads, tok_tile * P : (tok_tile + 1) * P, :].rearrange("h t d -> t h d"),
                 in_=result[:].rearrange("p (h d) -> p h d", d=HEAD),
@@ -248,8 +252,9 @@ def tile_stickyllamaattention_pa_kernel(
             for tok_tile in range(HALF_TILES):
                 one_pass(first[tok_tile], tok_tile, 0, 0, N_BLOCK, g)
         for tok_tile in range(HALF_TILES):
-            epilogue(first[tok_tile], tok_tile, 0, 0, N_BLOCK, nc.gpsimd)
+            finish(products(first[tok_tile], tok_tile, N_BLOCK), tok_tile, 0, 0, N_BLOCK, nc.gpsimd, nc.scalar)
 
+        held = None
         for half in range(2):
             for block in range(BLOCKS):
                 if half == 0 and block == 0:
@@ -264,5 +269,11 @@ def tile_stickyllamaattention_pa_kernel(
                         acc = psum.tile([P, width], F32, name="acc", tag="acc")
                         for g in range(PASSES):
                             one_pass(acc, tok_tile, block, c0, width, g)
-                        final = last and c0 + width == N_BLOCK
-                        epilogue(acc, tok_tile, block, c0, width, nc.vector if final else nc.gpsimd)
+                        pair = products(acc, tok_tile, width)
+                        if last and (c0, width) == TAIL_PIECES[-2]:
+                            held = (pair, c0, width)
+                        elif last and (c0, width) == TAIL_PIECES[-1]:
+                            finish(held[0], tok_tile, block, held[1], held[2], nc.vector, nc.scalar)
+                            finish(pair, tok_tile, block, c0, width, nc.vector, nc.sync)
+                        else:
+                            finish(pair, tok_tile, block, c0, width, nc.gpsimd, nc.scalar)

@@ -181,9 +181,9 @@ def tile_stickyllamaattention_pa_kernel(
         nc.vector.tensor_copy(out=whole_s[:], in_=turns[:])
         frac_s = small.tile(table_shape, F32, name="frac_s")
         nc.vector.tensor_tensor(out=frac_s[:], in0=turns[:], in1=whole_s[:], op=ALU.subtract)
-        signed_sin = small.tile([P, TILES, 2, HALF_D], F32, name="signed_sin")
-        nc.scalar.activation(out=signed_sin[:, :, 1, :], in_=frac_s[:], func=ACT.Sin, scale=2.0 * PI)
-        nc.scalar.activation(out=signed_sin[:, :, 0, :], in_=frac_s[:], func=ACT.Sin, scale=-2.0 * PI)
+        factors = small.tile([P, TILES, 2, 2, HALF_D], F32, name="factors")
+        nc.scalar.activation(out=factors[:, :, 1, 0, :], in_=frac_s[:], func=ACT.Sin, scale=2.0 * PI)
+        nc.scalar.activation(out=factors[:, :, 1, 1, :], in_=frac_s[:], func=ACT.Sin, scale=-2.0 * PI)
         whole_c = small.tile(table_shape, I32, name="whole_c")
         nc.vector.tensor_scalar(out=whole_c[:], in0=turns[:], scalar1=0.25, scalar2=None, op0=ALU.add)
         frac_c = small.tile(table_shape, F32, name="frac_c")
@@ -195,8 +195,8 @@ def tile_stickyllamaattention_pa_kernel(
             op0=ALU.add,
             op1=ALU.subtract,
         )
-        cos_t = small.tile(table_shape, F32, name="cos_t")
-        nc.scalar.activation(out=cos_t[:], in_=frac_c[:], func=ACT.Sin, scale=2.0 * PI)
+        nc.scalar.activation(out=factors[:, :, 0, 0, :], in_=frac_c[:], func=ACT.Sin, scale=2.0 * PI)
+        nc.scalar.activation(out=factors[:, :, 0, 1, :], in_=frac_c[:], func=ACT.Sin, scale=2.0 * PI)
 
         def one_pass(acc, tok_tile, block, c0, width, g):
             half, m_in = divmod(tok_tile, HALF_TILES)
@@ -212,29 +212,28 @@ def tile_stickyllamaattention_pa_kernel(
 
         def products(acc, tok_tile, width):
             heads = width // HEAD
-            x_halves = acc[:].rearrange("p (a d) -> p a d", d=HALF_D)
-            x_heads = acc[:].rearrange("p (h u d) -> p h u d", u=2, d=HALF_D)
-            direct = work.tile([P, width], F32, name="direct", tag="direct")
+            prod = work.tile([P, 2, width], F32, name="prod", tag="prod")
             nc.vector.tensor_tensor(
-                out=direct[:].rearrange("p (a d) -> p a d", d=HALF_D),
-                in0=x_halves,
-                in1=cos_t[:, tok_tile, :].unsqueeze(1).to_broadcast([P, 2 * heads, HALF_D]),
+                out=prod[:].rearrange("p r (h e) -> p r h e", e=HEAD),
+                in0=acc[:].rearrange("p (h e) -> p h e", e=HEAD).unsqueeze(1).to_broadcast([P, 2, heads, HEAD]),
+                in1=factors[:, tok_tile, :, :, :]
+                .rearrange("p r u d -> p r (u d)")
+                .unsqueeze(2)
+                .to_broadcast([P, 2, heads, HEAD]),
                 op=ALU.mult,
             )
-            crossed = work.tile([P, width], F32, name="crossed", tag="crossed")
-            nc.vector.tensor_tensor(
-                out=crossed[:].rearrange("p (h u d) -> p h u d", u=2, d=HALF_D),
-                in0=x_heads[:, :, ::-1, :],
-                in1=signed_sin[:, tok_tile, :, :].unsqueeze(1).to_broadcast([P, heads, 2, HALF_D]),
-                op=ALU.mult,
-            )
-            return direct, crossed
+            return prod
 
-        def finish(pair, tok_tile, block, c0, width, add_engine, store_queue):
+        def finish(prod, tok_tile, block, c0, width, add_engine, store_queue):
             heads = width // HEAD
-            direct, crossed = pair
+            halves = prod[:].rearrange("p r (h u d) -> p r h u d", u=2, d=HALF_D)
             result = work.tile([P, width], F32, name="result", tag="result", bufs=6)
-            add_engine.tensor_tensor(out=result[:], in0=direct[:], in1=crossed[:], op=ALU.add)
+            add_engine.tensor_tensor(
+                out=result[:].rearrange("p (h u d) -> p h u d", u=2, d=HALF_D),
+                in0=halves[:, 0, :, :, :],
+                in1=halves[:, 1, :, ::-1, :],
+                op=ALU.add,
+            )
             if block < Q_BLOCKS:
                 dest, h0 = out_0, (block * N_BLOCK + c0) // HEAD
             else:

@@ -99,7 +99,7 @@ def tile_stickyllamaattention_pa_kernel(
         nc.gpsimd.memset(zeros[:], 0.0)
 
         load_codes("w", 0, 0, 1)
-        load_codes("h", 0, 0, 1, 0, HALF_TOK // 4)
+        load_codes("h", 0, 0, 1, 0, P)
         g0, g1 = FIRST_RUNS[0]
         w_plane = make_plane("w", 0, g0, g1)
         h_plane = make_plane("h", 0, g0, g1)
@@ -107,7 +107,7 @@ def tile_stickyllamaattention_pa_kernel(
             load_scale_rows(w_plane, "w", 0, g0, g1, quad)
         for quad in range(4):
             load_scale_rows(h_plane, "h", 0, g0, g1, quad)
-        load_codes("h", 0, 0, 1, HALF_TOK // 4, HALF_TOK // 4)
+        load_codes("h", 0, 0, 1, P, HALF_TOK // 2 - P)
         load_codes("h", 0, 0, 1, HALF_TOK // 2, HALF_TOK // 2)
         for g in range(1, g1):
             load_codes("w", 0, g, g + 1)

from contextlib import ExitStack

import concourse.mybir as mybir

F32 = mybir.dt.float32
BF16 = mybir.dt.bfloat16
I32 = mybir.dt.int32
U8 = mybir.dt.uint8
FP4X4 = mybir.dt.float4_e2m1fn_x4
ALU = mybir.AluOpType
ACT = mybir.ActivationFunctionType

P = 128
TOKENS = 2048
HIDDEN = 4096
PASSES = HIDDEN // 512
HEAD = 128
HALF_D = HEAD // 2
N_BLOCK = 512
Q_BLOCKS = 4
BLOCKS = 5
TILES = TOKENS // P
HALF_TILES = 8
HALF_TOK = HALF_TILES * P

PI = 3.141592653589793
ROPE_BASE = 5.0e5

FLOPS = 2 * TOKENS * (BLOCKS * N_BLOCK) * HIDDEN

N_WARM = 8
FIRST_RUNS = ((0, 2), (2, 5), (5, 8))
TAIL_PIECES = ((0, 256), (256, 128), (384, 128))


def tile_stickyllamaattention_pa_kernel(
    tc,
    hidden_states_words,
    hidden_states_scales,
    wq_words,
    wq_scales,
    wk_words,
    wk_scales,
    out_0,
    out_1,
):
    nc = tc.nc

    with ExitStack() as ctx:
        keep = ctx.enter_context(tc.tile_pool(name="keep", bufs=1))
        small = ctx.enter_context(tc.tile_pool(name="small", bufs=1))
        work = ctx.enter_context(tc.tile_pool(name="work", bufs=4))
        psum = ctx.enter_context(tc.psum_pool(name="psum", bufs=8))
        ctx.enter_context(tc.manual_schedule())

        codes = {}
        planes = {}

        def source(kind, chunk):
            if kind == "h":
                return hidden_states_words, hidden_states_scales, chunk * HALF_TOK, HALF_TOK
            if chunk < Q_BLOCKS:
                return wq_words, wq_scales, chunk * N_BLOCK, N_BLOCK
            return wk_words, wk_scales, 0, N_BLOCK

        def make_plane(kind, chunk, g0, g1):
            cols = source(kind, chunk)[3]
            plane = keep.tile([P, g1 - g0, cols], U8, name="pl_%s%d_%d" % (kind, chunk, g0), align_bytes=256)
            nc.vector.memset(plane[:].rearrange("p g c -> p (g c)").bitcast(I32), 0)
            for g in range(g0, g1):
                planes[(kind, chunk, g)] = plane[:, g - g0, :]
            return plane

        def load_scale_rows(plane, kind, chunk, g0, g1, quad):
            scales, c0, cols = source(kind, chunk)[1:]
            nc.sync.dma_start(
                out=plane[32 * quad : 32 * quad + 4, :, :].bitcast(I32),
                in_=scales[g0:g1, 4 * quad : 4 * quad + 4, c0 : c0 + cols].rearrange("g r n -> r g n").bitcast(I32),
            )

        def load_codes(kind, chunk, g0, g1, first_col=0, n_cols=None):
            words, unused, c0, cols = source(kind, chunk)
            c0 += first_col
            if n_cols is not None:
                cols = n_cols
            tile = keep.tile([P, g1 - g0, 2 * cols], U8, name="cd_%s%d_%d_%d" % (kind, chunk, g0, first_col), align_bytes=256)
            nc.sync.dma_start(
                out=tile[:].bitcast(I32),
                in_=words[g0:g1, :, 2 * c0 : 2 * (c0 + cols)].rearrange("g p c -> p g c").bitcast(I32),
            )
            for g in range(g0, g1):
                if kind == "w":
                    codes[("w", chunk, g)] = tile[:, g - g0, :]
                else:
                    for i in range(cols // P):
                        codes[("h", c0 // P + i, g)] = tile[:, g - g0, 2 * P * i : 2 * P * (i + 1)]

        zeros = small.tile([P, N_BLOCK], BF16, name="zeros")
        nc.gpsimd.memset(zeros[:], 0.0)

        load_codes("w", 0, 0, 1)
        load_codes("h", 0, 0, 1, 0, P)
        g0, g1 = FIRST_RUNS[0]
        w_plane = make_plane("w", 0, g0, g1)
        h_plane = make_plane("h", 0, g0, g1)
        for quad in range(4):
            load_scale_rows(w_plane, "w", 0, g0, g1, quad)
        for quad in range(4):
            load_scale_rows(h_plane, "h", 0, g0, g1, quad)
        load_codes("h", 0, 0, 1, P, HALF_TOK // 2 - P)
        load_codes("h", 0, 0, 1, HALF_TOK // 2, HALF_TOK // 2)
        for g in range(1, g1):
            load_codes("w", 0, g, g + 1)
            load_codes("h", 0, g, g + 1)
        for g0, g1 in FIRST_RUNS[1:]:
            w_plane = make_plane("w", 0, g0, g1)
            h_plane = make_plane("h", 0, g0, g1)
            for quad in range(4):
                load_scale_rows(w_plane, "w", 0, g0, g1, quad)
            for quad in range(4):
                load_scale_rows(h_plane, "h", 0, g0, g1, quad)
            for g in range(g0, g1):
                load_codes("w", 0, g, g + 1)
                load_codes("h", 0, g, g + 1)

        warm = psum.tile([P, N_BLOCK], F32, name="warm", tag="acc")
        for i in range(N_WARM):
            nc.tensor.matmul(out=warm[:], lhsT=zeros[:, 0:P], rhs=zeros[:], start=True, stop=True)

        pos_i = small.tile([P, TILES], I32, name="pos_i")
        nc.gpsimd.iota(pos_i[:], pattern=[[P, TILES]], base=0, channel_multiplier=1)
        inv = small.tile([P, HALF_D], F32, name="inv")
        nc.vector.memset(inv[:, 0:1], 1.0)
        scratch = small.tile([P, 1], F32, name="scratch")
        nc.scalar.activation(out=scratch[:], in_=inv[:, 0:1], func=ACT.Sin)
        pos_f = small.tile([P, TILES], F32, name="pos_f")

        later = [("w", 1), ("w", 2), ("w", 3), ("w", 4), ("h", 1)]

        def load_later(kind, chunk):
            plane = make_plane(kind, chunk, 0, PASSES)
            for quad in range(4):
                load_scale_rows(plane, kind, chunk, 0, PASSES, quad)
            for g in range(0, PASSES, 4):
                load_codes(kind, chunk, g, g + 4)

        m = 1
        while m < HALF_D:
            nc.vector.tensor_scalar(
                out=inv[:, m : 2 * m], in0=inv[:, 0:m], scalar1=ROPE_BASE ** (-m / 64.0), scalar2=None, op0=ALU.mult
            )
            if later:
                kind, chunk = later[0]
                later.remove(later[0])
                load_later(kind, chunk)
            m *= 2
        nc.vector.tensor_copy(out=pos_f[:], in_=pos_i[:])
        smooth_raw = small.tile([P, HALF_D], F32, name="smooth_raw")
        nc.vector.tensor_scalar(
            out=smooth_raw[:], in0=inv[:], scalar1=8192.0 / (6.0 * PI), scalar2=-1.0 / 3.0, op0=ALU.mult, op1=ALU.add
        )
        smooth = small.tile([P, HALF_D], F32, name="smooth")
        nc.vector.tensor_scalar(out=smooth[:], in0=smooth_raw[:], scalar1=0.0, scalar2=1.0, op0=ALU.max, op1=ALU.min)
        gain = small.tile([P, HALF_D], F32, name="gain")
        nc.vector.tensor_scalar(
            out=gain[:], in0=smooth[:], scalar1=7.0 / (16.0 * PI), scalar2=1.0 / (16.0 * PI), op0=ALU.mult, op1=ALU.add
        )
        turns_per_pos = small.tile([P, HALF_D], F32, name="turns_per_pos")
        nc.vector.tensor_tensor(out=turns_per_pos[:], in0=inv[:], in1=gain[:], op=ALU.mult)

        table_shape = [P, TILES, HALF_D]
        turns = small.tile(table_shape, F32, name="turns")
        nc.vector.tensor_tensor(
            out=turns[:],
            in0=pos_f[:].unsqueeze(2).to_broadcast(table_shape),
            in1=turns_per_pos[:].unsqueeze(1).to_broadcast(table_shape),
            op=ALU.mult,
        )
        flat = "p i j -> p (i j)"
        whole_s = small.tile(table_shape, I32, name="whole_s")
        nc.vector.tensor_copy(out=whole_s[:], in_=turns[:])
        frac_s = small.tile(table_shape, F32, name="frac_s")
        nc.vector.tensor_tensor(out=frac_s[:], in0=turns[:], in1=whole_s[:], op=ALU.subtract)
        factors = small.tile([P, TILES, 2, 2, HALF_D], F32, name="factors")
        nc.scalar.activation(out=factors[:, :, 1, 0, :], in_=frac_s[:], func=ACT.Sin, scale=2.0 * PI)
        nc.scalar.activation(out=factors[:, :, 1, 1, :], in_=frac_s[:], func=ACT.Sin, scale=-2.0 * PI)
        whole_c = small.tile(table_shape, I32, name="whole_c")
        nc.vector.tensor_scalar(out=whole_c[:], in0=turns[:], scalar1=0.25, scalar2=None, op0=ALU.add)
        frac_c = small.tile(table_shape, F32, name="frac_c")
        nc.vector.scalar_tensor_tensor(
            out=frac_c[:].rearrange(flat),
            in0=turns[:].rearrange(flat),
            scalar=0.25,
            in1=whole_c[:].rearrange(flat),
            op0=ALU.add,
            op1=ALU.subtract,
        )
        nc.scalar.activation(out=factors[:, :, 0, 0, :], in_=frac_c[:], func=ACT.Sin, scale=2.0 * PI)
        nc.scalar.activation(out=factors[:, :, 0, 1, :], in_=frac_c[:], func=ACT.Sin, scale=2.0 * PI)

        def one_pass(acc, tok_tile, block, c0, width, g):
            half, m_in = divmod(tok_tile, HALF_TILES)
            nc.tensor.matmul_mx(
                out=acc[:],
                lhsT=codes[("h", tok_tile, g)].bitcast(FP4X4),
                lhsT_scale=planes[("h", half, g)][:, P * m_in : P * (m_in + 1)],
                rhs=codes[("w", block, g)][:, 2 * c0 : 2 * (c0 + width)].bitcast(FP4X4),
                rhs_scale=planes[("w", block, g)][:, c0 : c0 + width],
                start=(g == 0),
                stop=(g == PASSES - 1),
            )

        def products(acc, tok_tile, width):
            heads = width // HEAD
            prod = work.tile([P, 2, width], F32, name="prod", tag="prod")
            nc.vector.tensor_tensor(
                out=prod[:].rearrange("p r (h e) -> p r h e", e=HEAD),
                in0=acc[:].rearrange("p (h e) -> p h e", e=HEAD).unsqueeze(1).to_broadcast([P, 2, heads, HEAD]),
                in1=factors[:, tok_tile, :, :, :]
                .rearrange("p r u d -> p r (u d)")
                .unsqueeze(2)
                .to_broadcast([P, 2, heads, HEAD]),
                op=ALU.mult,
            )
            return prod

        def finish(prod, tok_tile, block, c0, width, add_engine, store_queue):
            heads = width // HEAD
            halves = prod[:].rearrange("p r (h u d) -> p r h u d", u=2, d=HALF_D)
            result = work.tile([P, width], F32, name="result", tag="result", bufs=6)
            add_engine.tensor_tensor(
                out=result[:].rearrange("p (h u d) -> p h u d", u=2, d=HALF_D),
                in0=halves[:, 0, :, :, :],
                in1=halves[:, 1, :, ::-1, :],
                op=ALU.add,
            )
            if block < Q_BLOCKS:
                dest, h0 = out_0, (block * N_BLOCK + c0) // HEAD
            else:
                dest, h0 = out_1, c0 // HEAD
            store_queue.dma_start(
                out=dest[0, h0 : h0 + heads, tok_tile * P : (tok_tile + 1) * P, :].rearrange("h t d -> t h d"),
                in_=result[:].rearrange("p (h d) -> p h d", d=HEAD),
            )

        first = []
        for tok_tile in range(HALF_TILES):
            acc = psum.tile([P, N_BLOCK], F32, name="acc%d" % tok_tile, tag="acc")
            first.append(acc)
        for g in range(PASSES):
            for tok_tile in range(HALF_TILES):
                one_pass(first[tok_tile], tok_tile, 0, 0, N_BLOCK, g)
        for tok_tile in range(HALF_TILES):
            finish(products(first[tok_tile], tok_tile, N_BLOCK), tok_tile, 0, 0, N_BLOCK, nc.gpsimd, nc.scalar)

        held = None
        for half in range(2):
            for block in range(BLOCKS):
                if half == 0 and block == 0:
                    continue
                for m_in in range(HALF_TILES):
                    tok_tile = half * HALF_TILES + m_in
                    last = half == 1 and block == BLOCKS - 1 and m_in == HALF_TILES - 1
                    pieces = TAIL_PIECES if last else ((0, N_BLOCK),)
                    if half == 1 and block == BLOCKS - 1 and m_in == HALF_TILES - 2:
                        pieces = ((0, 256), (256, 256))
                    for c0, width in pieces:
                        acc = psum.tile([P, width], F32, name="acc", tag="acc")
                        for g in range(PASSES):
                            one_pass(acc, tok_tile, block, c0, width, g)
                        pair = products(acc, tok_tile, width)
                        if last and (c0, width) == TAIL_PIECES[-2]:
                            held = (pair, c0, width)
                        elif last and (c0, width) == TAIL_PIECES[-1]:
                            finish(held[0], tok_tile, block, held[1], held[2], nc.vector, nc.scalar)
                            finish(pair, tok_tile, block, c0, width, nc.vector, nc.sync)
                        else:
                            finish(pair, tok_tile, block, c0, width, nc.gpsimd, nc.scalar)
